import numpy as np
import ml_dtypes


def mxq(x, axis, fmt="e4m3"):
    dtype, down = {"e4m3": (ml_dtypes.float8_e4m3fn, 7), "e5m2": (ml_dtypes.float8_e5m2, 14)}[fmt]
    v = np.moveaxis(np.asarray(x, np.float32).astype(ml_dtypes.bfloat16).astype(np.float64), axis, -1)
    blocks = v.reshape(v.shape[:-1] + (-1, 32))
    amax = np.abs(blocks).max(-1, keepdims=True)
    byte = np.maximum(np.where(amax > 0, np.frexp(amax)[1] - 1 + 127, 0) - down, 1)
    scale = np.exp2(byte - 127.0)
    codes = (blocks / scale).astype(np.float32).astype(dtype).astype(np.float64)
    return np.moveaxis((codes * scale).reshape(v.shape), -1, axis)


WIDE = False


def mx_kscale(k):
    if not WIDE:
        return np.ones(k)
    levels = np.array([10, -10, 5, -5, 0])
    a = np.random.permutation(np.resize(levels, k // 512 * 4)).reshape(k // 512, 4)
    idx = np.arange(k)
    return np.exp2(a[idx // 512, idx % 128 // 32])


BF16 = ml_dtypes.bfloat16


def bf(x):
    return np.asarray(x, np.float32).astype(BF16)


def f64(x):
    return np.asarray(x).astype(np.float64)


B, S, E, H, D = 4, 1024, 256, 8, 64
TD = 2 * D
K = H * TD
DEPTH = 12
LAMBDA_INIT = 0.8 - 0.6 * np.exp(-0.3 * DEPTH)
EPS = 1e-8
LS = 0.55 / D ** 0.25


def setup_inputs():
    t = mx_kscale(K)[:TD]
    tk = np.tile(t, H)
    return {'attn1': bf(np.random.standard_normal((B, S, H, TD)) * 0.7),
            'attn2': bf(np.random.standard_normal((B, S, H, TD)) * 0.7),
            'lambda_q1': bf(np.random.standard_normal(D) * LS),
            'lambda_k1': bf(np.random.standard_normal(D) * LS),
            'lambda_q2': bf(np.random.standard_normal(D) * LS),
            'lambda_k2': bf(np.random.standard_normal(D) * LS),
            'ln_w': bf((1.0 + 0.1 * np.random.standard_normal(TD)) * t),
            'ln_b': bf(0.1 * np.random.standard_normal(TD) * t),
            'Wo': bf(np.random.standard_normal((K, E)) * 2.0 / np.sqrt(K) / tk[:, None])}


def reference(attn1, attn2, lambda_q1, lambda_k1, lambda_q2, lambda_k2, ln_w, ln_b, Wo):
    lam = (np.exp(np.sum(f64(lambda_q1) * f64(lambda_k1)))
           - np.exp(np.sum(f64(lambda_q2) * f64(lambda_k2))) + LAMBDA_INIT)
    a = f64(attn1) - lam * f64(attn2)
    rms = 1.0 / np.sqrt(np.mean(a * a, axis=-1, keepdims=True) + EPS)
    a = a * rms * f64(ln_w) + f64(ln_b)
    a = a * (1.0 - LAMBDA_INIT)
    h = a.reshape(B, S, K)
    return mxq(h, 2, 'e4m3') @ mxq(f64(Wo), 0, 'e4m3')

@@ -1,0 +1,286 @@
+import math
+from contextlib import ExitStack
+
+import concourse.mybir as mybir
+from concourse.masks import make_identity
+
+F32 = mybir.dt.float32
+BF16 = mybir.dt.bfloat16
+U32 = mybir.dt.uint32
+U8 = mybir.dt.uint8
+FP8X4 = mybir.dt.float8_e4m3fn_x4
+ALU = mybir.AluOpType
+ACT = mybir.ActivationFunctionType
+AX = mybir.AxisListType
+
+P = 128
+H = 8
+D = 128
+K = H * D
+E = 256
+TOKENS = 4096
+NT = TOKENS // P
+L0 = 0.8 - 0.6 * math.exp(-0.3 * 12)
+EPS = 1e-8
+FLOPS = 2 * TOKENS * K * E
+CHUNKS = [1, 1, 2, 4, 4, 4, 4, 4, 4, 2, 1, 1]
+VD_EVERY = 4
+
+
+def tile_multiheadflashdiff_pb_t_kernel(
+    tc, attn1, attn2, lambda_q1, lambda_k1, lambda_q2, lambda_k2, ln_w, ln_b, Wo, out
+):
+    nc = tc.nc
+    x1_dram = attn1.rearrange("b s h d -> (b s) (h d)")
+    x2_dram = attn2.rearrange("b s h d -> (b s) (h d)")
+    out_dram = out.rearrange("b s e -> (b s) e")
+
+    where = []
+    starts = []
+    t0 = 0
+    for c, J in enumerate(CHUNKS):
+        starts.append(t0)
+        t0 += P * J
+        for j in range(J):
+            where.append((c, j))
+    assert len(where) == NT
+
+    with ExitStack() as ctx:
+        ctx.enter_context(tc.manual_schedule())
+        const = ctx.enter_context(tc.tile_pool(name="const", bufs=1))
+        xpool = ctx.enter_context(tc.tile_pool(name="xpool", bufs=1))
+        opool = ctx.enter_context(tc.tile_pool(name="opool", bufs=1))
+        apool = ctx.enter_context(tc.tile_pool(name="apool", bufs=4))
+        jpool = ctx.enter_context(tc.tile_pool(name="jpool", bufs=2))
+        stat = ctx.enter_context(tc.tile_pool(name="stat", bufs=4))
+        gpool = ctx.enter_context(tc.tile_pool(name="gpool", bufs=3))
+        qpool = ctx.enter_context(tc.tile_pool(name="qpool", bufs=3))
+        psum = ctx.enter_context(tc.psum_pool(name="psum", bufs=4))
+
+        zl = const.tile([P, 4 * 64], BF16, name="zl")
+        nc.vector.memset(zl[:], 0.0)
+        eps_t = const.tile([P, 1], F32, name="eps_t")
+        nc.vector.memset(eps_t[:], EPS)
+        ones = const.tile([P, P], BF16, name="ones")
+        nc.vector.memset(ones[:], 1.0)
+        zw = const.tile([P, P], BF16, name="zw")
+        nc.vector.memset(zw[:], 0.0)
+        ident = const.tile([P, P], F32, name="ident")
+        make_identity(nc, ident[:])
+        scr = const.tile([P, 2], F32, name="scr")
+        nc.scalar.activation(out=scr[:, 0:1], in_=eps_t[:], func=ACT.Exp)
+
+        for n, v in enumerate([lambda_q1, lambda_q2, lambda_k1, lambda_k2]):
+            nc.sync.dma_start(out=zl[0:1, n * 64 : (n + 1) * 64], in_=v.unsqueeze(0))
+        x1_sb = []
+        x2_sb = []
+        o_sb = []
+        wo_raw = const.tile([P, 2, 4, E], BF16, name="wo_raw")
+        for c, J in enumerate(CHUNKS):
+            rows = slice(starts[c], starts[c] + P * J)
+            x1c = xpool.tile([P, J, K], BF16, name="x1_%d" % c)
+            x2c = xpool.tile([P, J, K], BF16, name="x2_%d" % c)
+            nc.sync.dma_start(out=x2c[:], in_=x2_dram[rows, :].rearrange("(p j) k -> p j k", j=J))
+            nc.sync.dma_start(out=x1c[:], in_=x1_dram[rows, :].rearrange("(p j) k -> p j k", j=J))
+            x1_sb.append(x1c)
+            x2_sb.append(x2c)
+            o_sb.append(opool.tile([P, J, E], F32, name="o_%d" % c))
+            if c == 0:
+                nc.sync.dma_start(out=zw[0:1, :], in_=ln_w.unsqueeze(0))
+                nc.sync.dma_start(out=zw[1:2, :], in_=ln_b.unsqueeze(0))
+            if c == 1:
+                nc.sync.dma_start(
+                    out=wo_raw[:].rearrange("p g t n -> p (g t) n"),
+                    in_=Wo.rearrange("(c p) n -> p c n", p=P),
+                )
+
+        ps_l = psum.tile([P, 512], F32, tag="tp", name="ps_l")
+        nc.tensor.matmul(ps_l[:, 0:256], lhsT=ones[:], rhs=zl[:], start=True, stop=True)
+        qs = const.tile([P, 128], F32, name="qs")
+        nc.vector.tensor_copy(out=qs[:], in_=ps_l[:, 0:128])
+        prod = const.tile([P, 2, 64], F32, name="prod")
+        nc.vector.tensor_tensor(
+            out=prod[:].rearrange("p a b -> p (a b)"), in0=qs[:], in1=ps_l[:, 128:256], op=ALU.mult
+        )
+        dots = const.tile([P, 2], F32, name="dots")
+        nc.vector.tensor_reduce(out=dots[:], in_=prod[:], axis=AX.X, op=ALU.add)
+        ex = const.tile([P, 2], F32, name="ex")
+        nc.scalar.activation(out=ex[:], in_=dots[:], func=ACT.Exp)
+        nc.scalar.activation(out=scr[:, 1:2], in_=eps_t[:], func=ACT.Sqrt)
+        neglam = const.tile([P, 1], F32, name="neglam")
+        nc.vector.scalar_tensor_tensor(
+            out=neglam[:], in0=ex[:, 1:2], scalar=-L0, in1=ex[:, 0:1], op0=ALU.add, op1=ALU.subtract
+        )
+
+        identb = const.tile([P, P], BF16, name="identb")
+        wb = const.tile([P, 2], F32, name="wb")
+        wo_g = const.tile([P, 2, E, 4], BF16, name="wo_g", align_bytes=64)
+        wo_c = const.tile([P, 2 * E], U32, name="wo_c", align_bytes=64)
+        wo_s = const.tile([P, 2 * E], U8, name="wo_s", align_bytes=64)
+
+        def prep_wb():
+            nc.vector.tensor_copy(out=identb[:], in_=ident[:])
+            ps_w = psum.tile([P, P], BF16, tag="tp", name="ps_w")
+            nc.tensor.transpose(ps_w[:], zw[:], identb[:])
+            nc.vector.tensor_scalar(out=wb[:], in0=ps_w[:, 0:2], scalar1=1.0 - L0, scalar2=None, op0=ALU.mult)
+
+        def prep_wo_group():
+            nc.vector.tensor_copy(out=wo_g[:], in_=wo_raw[:].rearrange("p g t n -> p g n t"))
+
+        def prep_wo_quant():
+            nc.vector.quantize_mx(
+                out=wo_c[:].bitcast(FP8X4), scales=wo_s[:], in_=wo_g[:].rearrange("p g n t -> p (g n t)")
+            )
+
+        a_t = {}
+        ss_t = {}
+        rt_t = {}
+        r_t = {}
+        pt_t = {}
+        grp_t = {}
+        q_t = {}
+        po_t = {}
+
+        def ok(i):
+            return 0 <= i < NT
+
+        def st_a(i):
+            if not ok(i):
+                return
+            c, j = where[i]
+            a = apool.tile([P, K], F32, tag="a", name="a_%d" % i)
+            a_t[i] = a
+            pieces = 4 if i == 0 else 1
+            w = K // pieces
+            for s in range(pieces):
+                cols = slice(s * w, (s + 1) * w)
+                nc.vector.scalar_tensor_tensor(
+                    out=a[:, cols],
+                    in0=x2_sb[c][:, j, cols],
+                    scalar=neglam[:, 0:1],
+                    in1=x1_sb[c][:, j, cols],
+                    op0=ALU.mult,
+                    op1=ALU.add,
+                )
+
+        def st_b(i):
+            if not ok(i):
+                return
+            ss = stat.tile([P, H], F32, tag="ss", name="ss_%d" % i)
+            ss_t[i] = ss
+            junk = jpool.tile([P, K], BF16, tag="junk", name="junk_%d" % i)
+            for h in range(H):
+                cols = slice(h * D, (h + 1) * D)
+                nc.scalar.activation(
+                    out=junk[:, cols], in_=a_t[i][:, cols], func=ACT.Square, accum_out=ss[:, h : h + 1]
+                )
+
+        def st_sqrt(i):
+            if not ok(i):
+                return
+            rt = stat.tile([P, H], F32, tag="rt", name="rt_%d" % i)
+            rt_t[i] = rt
+            nc.scalar.activation(out=rt[:], in_=ss_t[i][:], func=ACT.Sqrt, scale=1.0 / D, bias=eps_t[:, 0:1])
+
+        def st_recip(i):
+            if not ok(i):
+                return
+            r = stat.tile([P, H], F32, tag="r", name="r_%d" % i)
+            r_t[i] = r
+            nc.vector.reciprocal(out=r[:], in_=rt_t[i][:])
+
+        def st_c(i):
+            if not ok(i):
+                return
+            a = a_t[i]
+            for h in range(H):
+                cols = slice(h * D, (h + 1) * D)
+                nc.vector.tensor_scalar(
+                    out=a[:, cols], in0=a[:, cols], scalar1=r_t[i][:, h : h + 1], scalar2=None, op0=ALU.mult
+                )
+
+        def st_t(i):
+            if not ok(i):
+                return
+            for g in range(2):
+                pt = psum.tile([P, 4, P], F32, tag="tp", name="pt_%d_%d" % (i, g))
+                pt_t[(i, g)] = pt
+                for t in range(4):
+                    h = 4 * g + t
+                    nc.tensor.transpose(pt[:, t, :], a_t[i][:, h * D : (h + 1) * D], ident[:])
+
+        def st_d(i, g):
+            if not ok(i):
+                return
+            if g == 0:
+                grp_t[i] = gpool.tile([P, 2, P, 4], BF16, tag="grp", name="grp_%d" % i, align_bytes=64)
+            dst = grp_t[i][:, g, :, :]
+            src = pt_t[(i, g)][:].rearrange("p t r -> p r t")
+            if g == 1 and (i % VD_EVERY == VD_EVERY - 1 or i == NT - 1):
+                nc.vector.tensor_scalar(
+                    out=dst, in0=src, scalar1=wb[:, 0:1], scalar2=wb[:, 1:2], op0=ALU.mult, op1=ALU.add
+                )
+            else:
+                nc.scalar.activation(out=dst, in_=src, func=ACT.Identity, scale=wb[:, 0:1], bias=wb[:, 1:2])
+
+        def st_q(i):
+            if not ok(i):
+                return
+            codes = qpool.tile([P, 2 * P], U32, tag="codes", name="codes_%d" % i, align_bytes=64)
+            sc = qpool.tile([P, 2 * P], U8, tag="sc", name="sc_%d" % i, align_bytes=64)
+            q_t[i] = (codes, sc)
+            nc.vector.quantize_mx(
+                out=codes[:].bitcast(FP8X4), scales=sc[:], in_=grp_t[i][:].rearrange("p g r t -> p (g r t)")
+            )
+
+        def st_m(i):
+            if not ok(i):
+                return
+            c, j = where[i]
+            if j % 2 == 0:
+                po_t[(c, j // 2)] = psum.tile([P, 2, E], F32, tag="po", bufs=2, name="po_%d" % i)
+            po = po_t[(c, j // 2)]
+            codes, sc = q_t[i]
+            for g in range(2):
+                nc.tensor.matmul_mx(
+                    out=po[:, j % 2, :],
+                    lhsT=codes[:, g * P : (g + 1) * P].bitcast(FP8X4),
+                    lhsT_scale=sc[:, g * P : (g + 1) * P],
+                    rhs=wo_c[:, g * E : (g + 1) * E].bitcast(FP8X4),
+                    rhs_scale=wo_s[:, g * E : (g + 1) * E],
+                    start=(g == 0),
+                    stop=(g == 1),
+                )
+
+        def st_e(i):
+            if not ok(i):
+                return
+            c, j = where[i]
+            J = CHUNKS[c]
+            if j % 2 == 0 and j != J - 1:
+                return
+            j0 = j - (j % 2)
+            n = j - j0 + 1
+            nc.vector.tensor_copy(out=o_sb[c][:, j0 : j0 + n, :], in_=po_t[(c, j // 2)][:, 0:n, :])
+            if j == J - 1:
+                rows = slice(starts[c], starts[c] + P * J)
+                nc.sync.dma_start(out=out_dram[rows, :].rearrange("(p j) e -> p j e", j=J), in_=o_sb[c][:])
+
+        for t in range(-1, NT + 5):
+            st_recip(t - 1)
+            st_a(t + 1)
+            if t == -1:
+                prep_wb()
+            if t == 0:
+                prep_wo_group()
+            st_b(t)
+            st_d(t - 2, 0)
+            st_sqrt(t)
+            st_d(t - 2, 1)
+            st_c(t - 1)
+            st_t(t - 1)
+            if t == 1:
+                prep_wo_quant()
+            st_q(t - 3)
+            st_m(t - 3)
+            st_e(t - 4)

@@ -24,7 +24,7 @@ L0 = 0.8 - 0.6 * math.exp(-0.3 * 12)
 EPS = 1e-8
 FLOPS = 2 * TOKENS * K * E
 CHUNKS = [1, 1, 2, 4, 4, 4, 4, 4, 4, 2, 1, 1]
-VD_EVERY = 4
+VD_EVERY = 2
 
 
 def tile_multiheadflashdiff_pb_t_kernel(
@@ -57,12 +57,9 @@ def tile_multiheadflashdiff_pb_t_kernel(
         qpool = ctx.enter_context(tc.tile_pool(name="qpool", bufs=3))
         psum = ctx.enter_context(tc.psum_pool(name="psum", bufs=4))
 
-        zl = const.tile([P, 4 * 64], BF16, name="zl")
-        nc.vector.memset(zl[:], 0.0)
+        lamv = const.tile([P, 4 * 64], BF16, name="lamv")
         eps_t = const.tile([P, 1], F32, name="eps_t")
         nc.vector.memset(eps_t[:], EPS)
-        ones = const.tile([P, P], BF16, name="ones")
-        nc.vector.memset(ones[:], 1.0)
         zw = const.tile([P, P], BF16, name="zw")
         nc.vector.memset(zw[:], 0.0)
         ident = const.tile([P, P], F32, name="ident")
@@ -71,7 +68,7 @@ def tile_multiheadflashdiff_pb_t_kernel(
         nc.scalar.activation(out=scr[:, 0:1], in_=eps_t[:], func=ACT.Exp)
 
         for n, v in enumerate([lambda_q1, lambda_q2, lambda_k1, lambda_k2]):
-            nc.sync.dma_start(out=zl[0:1, n * 64 : (n + 1) * 64], in_=v.unsqueeze(0))
+            nc.sync.dma_start(out=lamv[:, n * 64 : (n + 1) * 64], in_=v.partition_broadcast(P))
         x1_sb = []
         x2_sb = []
         o_sb = []
@@ -80,8 +77,11 @@ def tile_multiheadflashdiff_pb_t_kernel(
             rows = slice(starts[c], starts[c] + P * J)
             x1c = xpool.tile([P, J, K], BF16, name="x1_%d" % c)
             x2c = xpool.tile([P, J, K], BF16, name="x2_%d" % c)
-            nc.sync.dma_start(out=x2c[:], in_=x2_dram[rows, :].rearrange("(p j) k -> p j k", j=J))
-            nc.sync.dma_start(out=x1c[:], in_=x1_dram[rows, :].rearrange("(p j) k -> p j k", j=J))
+            halves = 2 if c == 0 else 1
+            for s in range(halves):
+                cols = slice(s * K // halves, (s + 1) * K // halves)
+                nc.sync.dma_start(out=x2c[:, :, cols], in_=x2_dram[rows, cols].rearrange("(p j) k -> p j k", j=J))
+                nc.sync.dma_start(out=x1c[:, :, cols], in_=x1_dram[rows, cols].rearrange("(p j) k -> p j k", j=J))
             x1_sb.append(x1c)
             x2_sb.append(x2c)
             o_sb.append(opool.tile([P, J, E], F32, name="o_%d" % c))
@@ -94,19 +94,15 @@ def tile_multiheadflashdiff_pb_t_kernel(
                     in_=Wo.rearrange("(c p) n -> p c n", p=P),
                 )
 
-        ps_l = psum.tile([P, 512], F32, tag="tp", name="ps_l")
-        nc.tensor.matmul(ps_l[:, 0:256], lhsT=ones[:], rhs=zl[:], start=True, stop=True)
-        qs = const.tile([P, 128], F32, name="qs")
-        nc.vector.tensor_copy(out=qs[:], in_=ps_l[:, 0:128])
         prod = const.tile([P, 2, 64], F32, name="prod")
         nc.vector.tensor_tensor(
-            out=prod[:].rearrange("p a b -> p (a b)"), in0=qs[:], in1=ps_l[:, 128:256], op=ALU.mult
+            out=prod[:].rearrange("p a b -> p (a b)"), in0=lamv[:, 0:128], in1=lamv[:, 128:256], op=ALU.mult
         )
         dots = const.tile([P, 2], F32, name="dots")
         nc.vector.tensor_reduce(out=dots[:], in_=prod[:], axis=AX.X, op=ALU.add)
         ex = const.tile([P, 2], F32, name="ex")
         nc.scalar.activation(out=ex[:], in_=dots[:], func=ACT.Exp)
-        nc.scalar.activation(out=scr[:, 1:2], in_=eps_t[:], func=ACT.Sqrt)
+        nc.scalar.activation(out=scr[:, 1:2], in_=eps_t[:], func=ACT.Abs_reciprocal_sqrt)
         neglam = const.tile([P, 1], F32, name="neglam")
         nc.vector.scalar_tensor_tensor(
             out=neglam[:], in0=ex[:, 1:2], scalar=-L0, in1=ex[:, 0:1], op0=ALU.add, op1=ALU.subtract
@@ -134,7 +130,6 @@ def tile_multiheadflashdiff_pb_t_kernel(
 
         a_t = {}
         ss_t = {}
-        rt_t = {}
         r_t = {}
         pt_t = {}
         grp_t = {}
@@ -178,16 +173,11 @@ def tile_multiheadflashdiff_pb_t_kernel(
         def st_sqrt(i):
             if not ok(i):
                 return
-            rt = stat.tile([P, H], F32, tag="rt", name="rt_%d" % i)
-            rt_t[i] = rt
-            nc.scalar.activation(out=rt[:], in_=ss_t[i][:], func=ACT.Sqrt, scale=1.0 / D, bias=eps_t[:, 0:1])
-
-        def st_recip(i):
-            if not ok(i):
-                return
             r = stat.tile([P, H], F32, tag="r", name="r_%d" % i)
             r_t[i] = r
-            nc.vector.reciprocal(out=r[:], in_=rt_t[i][:])
+            nc.scalar.activation(
+                out=r[:], in_=ss_t[i][:], func=ACT.Abs_reciprocal_sqrt, scale=1.0 / D, bias=eps_t[:, 0:1]
+            )
 
         def st_c(i):
             if not ok(i):
@@ -267,7 +257,6 @@ def tile_multiheadflashdiff_pb_t_kernel(
                 nc.sync.dma_start(out=out_dram[rows, :].rearrange("(p j) e -> p j e", j=J), in_=o_sb[c][:])
 
         for t in range(-1, NT + 5):
-            st_recip(t - 1)
             st_a(t + 1)
             if t == -1:
                 prep_wb()

@@ -24,7 +24,7 @@ L0 = 0.8 - 0.6 * math.exp(-0.3 * 12)
 EPS = 1e-8
 FLOPS = 2 * TOKENS * K * E
 CHUNKS = [1, 1, 2, 4, 4, 4, 4, 4, 4, 2, 1, 1]
-VD_EVERY = 2
+VD_EVERY = 5
 
 
 def tile_multiheadflashdiff_pb_t_kernel(
@@ -57,9 +57,12 @@ def tile_multiheadflashdiff_pb_t_kernel(
         qpool = ctx.enter_context(tc.tile_pool(name="qpool", bufs=3))
         psum = ctx.enter_context(tc.psum_pool(name="psum", bufs=4))
 
-        lamv = const.tile([P, 4 * 64], BF16, name="lamv")
+        zl = const.tile([P, 4 * 64], BF16, name="zl")
+        nc.vector.memset(zl[:], 0.0)
         eps_t = const.tile([P, 1], F32, name="eps_t")
         nc.vector.memset(eps_t[:], EPS)
+        ones = const.tile([P, P], BF16, name="ones")
+        nc.vector.memset(ones[:], 1.0)
         zw = const.tile([P, P], BF16, name="zw")
         nc.vector.memset(zw[:], 0.0)
         ident = const.tile([P, P], F32, name="ident")
@@ -68,7 +71,7 @@ def tile_multiheadflashdiff_pb_t_kernel(
         nc.scalar.activation(out=scr[:, 0:1], in_=eps_t[:], func=ACT.Exp)
 
         for n, v in enumerate([lambda_q1, lambda_q2, lambda_k1, lambda_k2]):
-            nc.sync.dma_start(out=lamv[:, n * 64 : (n + 1) * 64], in_=v.partition_broadcast(P))
+            nc.sync.dma_start(out=zl[0:1, n * 64 : (n + 1) * 64], in_=v.unsqueeze(0))
         x1_sb = []
         x2_sb = []
         o_sb = []
@@ -94,9 +97,13 @@ def tile_multiheadflashdiff_pb_t_kernel(
                     in_=Wo.rearrange("(c p) n -> p c n", p=P),
                 )
 
+        ps_l = psum.tile([P, 512], F32, tag="tp", name="ps_l")
+        nc.tensor.matmul(ps_l[:, 0:256], lhsT=ones[:], rhs=zl[:], start=True, stop=True)
+        qs = const.tile([P, 128], F32, name="qs")
+        nc.vector.tensor_copy(out=qs[:], in_=ps_l[:, 0:128])
         prod = const.tile([P, 2, 64], F32, name="prod")
         nc.vector.tensor_tensor(
-            out=prod[:].rearrange("p a b -> p (a b)"), in0=lamv[:, 0:128], in1=lamv[:, 128:256], op=ALU.mult
+            out=prod[:].rearrange("p a b -> p (a b)"), in0=qs[:], in1=ps_l[:, 128:256], op=ALU.mult
         )
         dots = const.tile([P, 2], F32, name="dots")
         nc.vector.tensor_reduce(out=dots[:], in_=prod[:], axis=AX.X, op=ALU.add)

@@ -23,8 +23,9 @@ NT = TOKENS // P
 L0 = 0.8 - 0.6 * math.exp(-0.3 * 12)
 EPS = 1e-8
 FLOPS = 2 * TOKENS * K * E
-CHUNKS = [1, 1, 2, 4, 4, 4, 4, 4, 4, 2, 1, 1]
+CHUNKS = [1, 1, 1, 1, 2, 2, 4, 4, 4, 4, 4, 2, 1, 1]
 VD_EVERY = 5
+VD_TAIL = 28
 
 
 def tile_multiheadflashdiff_pb_t_kernel(
@@ -57,21 +58,34 @@ def tile_multiheadflashdiff_pb_t_kernel(
         qpool = ctx.enter_context(tc.tile_pool(name="qpool", bufs=3))
         psum = ctx.enter_context(tc.psum_pool(name="psum", bufs=4))
 
-        zl = const.tile([P, 4 * 64], BF16, name="zl")
-        nc.vector.memset(zl[:], 0.0)
-        eps_t = const.tile([P, 1], F32, name="eps_t")
-        nc.vector.memset(eps_t[:], EPS)
-        ones = const.tile([P, P], BF16, name="ones")
-        nc.vector.memset(ones[:], 1.0)
         zw = const.tile([P, P], BF16, name="zw")
         nc.vector.memset(zw[:], 0.0)
+        zl = const.tile([P, 2 * 64], BF16, name="zl")
+        ex = const.tile([P, 1], F32, name="ex")
+        nc.vector.memset(ex[:], 0.0)
+        nc.vector.memset(ex[32:33, :], 1.0)
+        sgn = const.tile([P, P], F32, name="sgn")
+        nc.vector.memset(sgn[:], 0.0)
+        nc.vector.tensor_scalar(
+            out=sgn[32:33, :], in0=sgn[32:33, :], scalar1=-L0, scalar2=None, op0=ALU.add
+        )
+        nc.vector.memset(sgn[0:2, :], 1.0)
+        nc.vector.memset(sgn[0:1, :], -1.0)
+        eps_t = const.tile([P, 1], F32, name="eps_t")
+        nc.vector.memset(eps_t[:], EPS)
         ident = const.tile([P, P], F32, name="ident")
         make_identity(nc, ident[:])
+        identb = const.tile([P, P], BF16, name="identb")
+        nc.vector.tensor_copy(out=identb[:], in_=ident[:])
+        wb = const.tile([P, 2], F32, name="wb")
         scr = const.tile([P, 2], F32, name="scr")
-        nc.scalar.activation(out=scr[:, 0:1], in_=eps_t[:], func=ACT.Exp)
 
         for n, v in enumerate([lambda_q1, lambda_q2, lambda_k1, lambda_k2]):
-            nc.sync.dma_start(out=zl[0:1, n * 64 : (n + 1) * 64], in_=v.unsqueeze(0))
+            row, col = n % 2, 64 * (n // 2)
+            nc.scalar.dma_start(out=zl[row : row + 1, col : col + 64], in_=v.unsqueeze(0))
+        nc.scalar.activation(out=scr[:, 0:1], in_=eps_t[:], func=ACT.Exp)
+        nc.scalar.dma_start(out=zw[0:1, :], in_=ln_w.unsqueeze(0))
+        nc.scalar.dma_start(out=zw[1:2, :], in_=ln_b.unsqueeze(0))
         x1_sb = []
         x2_sb = []
         o_sb = []
@@ -88,47 +102,38 @@ def tile_multiheadflashdiff_pb_t_kernel(
             x1_sb.append(x1c)
             x2_sb.append(x2c)
             o_sb.append(opool.tile([P, J, E], F32, name="o_%d" % c))
-            if c == 0:
-                nc.sync.dma_start(out=zw[0:1, :], in_=ln_w.unsqueeze(0))
-                nc.sync.dma_start(out=zw[1:2, :], in_=ln_b.unsqueeze(0))
-            if c == 1:
+            if c == 2:
                 nc.sync.dma_start(
                     out=wo_raw[:].rearrange("p g t n -> p (g t) n"),
                     in_=Wo.rearrange("(c p) n -> p c n", p=P),
                 )
 
-        ps_l = psum.tile([P, 512], F32, tag="tp", name="ps_l")
-        nc.tensor.matmul(ps_l[:, 0:256], lhsT=ones[:], rhs=zl[:], start=True, stop=True)
-        qs = const.tile([P, 128], F32, name="qs")
-        nc.vector.tensor_copy(out=qs[:], in_=ps_l[:, 0:128])
-        prod = const.tile([P, 2, 64], F32, name="prod")
-        nc.vector.tensor_tensor(
-            out=prod[:].rearrange("p a b -> p (a b)"), in0=qs[:], in1=ps_l[:, 128:256], op=ALU.mult
-        )
-        dots = const.tile([P, 2], F32, name="dots")
-        nc.vector.tensor_reduce(out=dots[:], in_=prod[:], axis=AX.X, op=ALU.add)
-        ex = const.tile([P, 2], F32, name="ex")
-        nc.scalar.activation(out=ex[:], in_=dots[:], func=ACT.Exp)
-        nc.scalar.activation(out=scr[:, 1:2], in_=eps_t[:], func=ACT.Abs_reciprocal_sqrt)
-        neglam = const.tile([P, 1], F32, name="neglam")
+        prod = const.tile([P, 64], F32, name="prod")
+        dots = const.tile([P, 1], F32, name="dots")
         nc.vector.scalar_tensor_tensor(
-            out=neglam[:], in0=ex[:, 1:2], scalar=-L0, in1=ex[:, 0:1], op0=ALU.add, op1=ALU.subtract
+            out=prod[0:2, :],
+            in0=zl[0:2, 0:64],
+            scalar=1.0,
+            in1=zl[0:2, 64:128],
+            op0=ALU.mult,
+            op1=ALU.mult,
+            accum_out=dots[0:2, :],
         )
+        nc.scalar.activation(out=ex[0:2, :], in_=dots[0:2, :], func=ACT.Exp)
+        nc.scalar.activation(out=scr[:, 1:2], in_=eps_t[:], func=ACT.Abs_reciprocal_sqrt)
+        ps_l = psum.tile([P, 1], F32, tag="tp", name="ps_l")
+        nc.tensor.matmul(ps_l[:], lhsT=sgn[:], rhs=ex[:], start=True, stop=True)
+        neglam = const.tile([P, 1], F32, name="neglam")
 
-        identb = const.tile([P, P], BF16, name="identb")
-        wb = const.tile([P, 2], F32, name="wb")
         wo_g = const.tile([P, 2, E, 4], BF16, name="wo_g", align_bytes=64)
         wo_c = const.tile([P, 2 * E], U32, name="wo_c", align_bytes=64)
         wo_s = const.tile([P, 2 * E], U8, name="wo_s", align_bytes=64)
 
-        def prep_wb():
-            nc.vector.tensor_copy(out=identb[:], in_=ident[:])
-            ps_w = psum.tile([P, P], BF16, tag="tp", name="ps_w")
-            nc.tensor.transpose(ps_w[:], zw[:], identb[:])
-            nc.vector.tensor_scalar(out=wb[:], in0=ps_w[:, 0:2], scalar1=1.0 - L0, scalar2=None, op0=ALU.mult)
+        ps_w = psum.tile([P, P], BF16, tag="tp", name="ps_w")
+        nc.tensor.transpose(ps_w[:], zw[:], identb[:])
 
-        def prep_wo_group():
-            nc.vector.tensor_copy(out=wo_g[:], in_=wo_raw[:].rearrange("p g t n -> p g n t"))
+        def prep_wo_group(g):
+            nc.vector.tensor_copy(out=wo_g[:, g], in_=wo_raw[:, g].rearrange("p t n -> p n t"))
 
         def prep_wo_quant():
             nc.vector.quantize_mx(
@@ -159,7 +164,7 @@ def tile_multiheadflashdiff_pb_t_kernel(
                 nc.vector.scalar_tensor_tensor(
                     out=a[:, cols],
                     in0=x2_sb[c][:, j, cols],
-                    scalar=neglam[:, 0:1],
+                    scalar=ps_l[:, 0:1] if i == 0 else neglam[:, 0:1],
                     in1=x1_sb[c][:, j, cols],
                     op0=ALU.mult,
                     op1=ALU.add,
@@ -213,7 +218,7 @@ def tile_multiheadflashdiff_pb_t_kernel(
                 grp_t[i] = gpool.tile([P, 2, P, 4], BF16, tag="grp", name="grp_%d" % i, align_bytes=64)
             dst = grp_t[i][:, g, :, :]
             src = pt_t[(i, g)][:].rearrange("p t r -> p r t")
-            if g == 1 and (i % VD_EVERY == VD_EVERY - 1 or i == NT - 1):
+            if g == 1 and (i % VD_EVERY == VD_EVERY - 1 or i >= VD_TAIL):
                 nc.vector.tensor_scalar(
                     out=dst, in0=src, scalar1=wb[:, 0:1], scalar2=wb[:, 1:2], op0=ALU.mult, op1=ALU.add
                 )
@@ -228,6 +233,19 @@ def tile_multiheadflashdiff_pb_t_kernel(
             q_t[i] = (codes, sc)
             nc.vector.quantize_mx(
                 out=codes[:].bitcast(FP8X4), scales=sc[:], in_=grp_t[i][:].rearrange("p g r t -> p (g r t)")
+            )
+
+        def st_qh(i, g):
+            if g == 0:
+                q_t[i] = (
+                    qpool.tile([P, 2 * P], U32, tag="codes", name="codes_%d" % i, align_bytes=64),
+                    qpool.tile([P, 2 * P], U8, tag="sc", name="sc_%d" % i, align_bytes=64),
+                )
+            codes, sc = q_t[i]
+            nc.vector.quantize_mx(
+                out=codes[:, g * P : (g + 1) * P].bitcast(FP8X4),
+                scales=sc[:, g * P : (g + 1) * P],
+                in_=grp_t[i][:, g].rearrange("p r t -> p (r t)"),
             )
 
         def st_m(i):
@@ -249,7 +267,7 @@ def tile_multiheadflashdiff_pb_t_kernel(
                     stop=(g == 1),
                 )
 
-        def st_e(i):
+        def st_e(i, copy=nc.vector.tensor_copy):
             if not ok(i):
                 return
             c, j = where[i]
@@ -258,25 +276,49 @@ def tile_multiheadflashdiff_pb_t_kernel(
                 return
             j0 = j - (j % 2)
             n = j - j0 + 1
-            nc.vector.tensor_copy(out=o_sb[c][:, j0 : j0 + n, :], in_=po_t[(c, j // 2)][:, 0:n, :])
+            copy(out=o_sb[c][:, j0 : j0 + n, :], in_=po_t[(c, j // 2)][:, 0:n, :])
             if j == J - 1:
                 rows = slice(starts[c], starts[c] + P * J)
                 nc.sync.dma_start(out=out_dram[rows, :].rearrange("(p j) e -> p j e", j=J), in_=o_sb[c][:])
 
-        for t in range(-1, NT + 5):
+        for t in range(-1, NT):
             st_a(t + 1)
             if t == -1:
-                prep_wb()
-            if t == 0:
-                prep_wo_group()
+                nc.vector.tensor_copy(out=neglam[:], in_=ps_l[:])
+            if t == 1:
+                nc.vector.tensor_scalar(out=wb[:], in0=ps_w[:, 0:2], scalar1=1.0 - L0, scalar2=None, op0=ALU.mult)
             st_b(t)
             st_d(t - 2, 0)
             st_sqrt(t)
             st_d(t - 2, 1)
             st_c(t - 1)
             st_t(t - 1)
-            if t == 1:
+            if t == 2:
+                prep_wo_group(0)
+            if t == 3:
+                prep_wo_group(1)
+            if t == 4:
                 prep_wo_quant()
             st_q(t - 3)
-            st_m(t - 3)
-            st_e(t - 4)
+            st_m(t - 4)
+            st_e(t - 5)
+        y, z = NT - 2, NT - 1
+        st_c(z)
+        st_t(z)
+        st_m(z - 3)
+        st_d(y, 0)
+        st_q(z - 2)
+        st_d(y, 1)
+        st_m(z - 2)
+        st_e(z - 4)
+        st_d(z, 0)
+        st_q(y)
+        st_m(y)
+        st_e(z - 3, nc.scalar.copy)
+        st_qh(z, 0)
+        st_d(z, 1)
+        st_e(z - 2, nc.scalar.copy)
+        st_qh(z, 1)
+        st_m(z)
+        st_e(y, nc.scalar.copy)
+        st_e(z)

@@ -24,8 +24,7 @@ L0 = 0.8 - 0.6 * math.exp(-0.3 * 12)
 EPS = 1e-8
 FLOPS = 2 * TOKENS * K * E
 CHUNKS = [1, 1, 1, 1, 2, 2, 4, 4, 4, 4, 4, 2, 1, 1]
-VD_EVERY = 5
-VD_TAIL = 28
+VD_EVERY = 4
 
 
 def tile_multiheadflashdiff_pb_t_kernel(
@@ -58,6 +57,8 @@ def tile_multiheadflashdiff_pb_t_kernel(
         qpool = ctx.enter_context(tc.tile_pool(name="qpool", bufs=3))
         psum = ctx.enter_context(tc.psum_pool(name="psum", bufs=4))
 
+        eps_t = const.tile([P, 1], F32, name="eps_t")
+        nc.vector.memset(eps_t[:], EPS)
         zw = const.tile([P, P], BF16, name="zw")
         nc.vector.memset(zw[:], 0.0)
         zl = const.tile([P, 2 * 64], BF16, name="zl")
@@ -71,8 +72,6 @@ def tile_multiheadflashdiff_pb_t_kernel(
         )
         nc.vector.memset(sgn[0:2, :], 1.0)
         nc.vector.memset(sgn[0:1, :], -1.0)
-        eps_t = const.tile([P, 1], F32, name="eps_t")
-        nc.vector.memset(eps_t[:], EPS)
         ident = const.tile([P, P], F32, name="ident")
         make_identity(nc, ident[:])
         identb = const.tile([P, P], BF16, name="identb")
@@ -82,7 +81,8 @@ def tile_multiheadflashdiff_pb_t_kernel(
 
         for n, v in enumerate([lambda_q1, lambda_q2, lambda_k1, lambda_k2]):
             row, col = n % 2, 64 * (n // 2)
-            nc.scalar.dma_start(out=zl[row : row + 1, col : col + 64], in_=v.unsqueeze(0))
+            queue = nc.sync if row == 0 else nc.scalar
+            queue.dma_start(out=zl[row : row + 1, col : col + 64], in_=v.unsqueeze(0))
         nc.scalar.activation(out=scr[:, 0:1], in_=eps_t[:], func=ACT.Exp)
         nc.scalar.dma_start(out=zw[0:1, :], in_=ln_w.unsqueeze(0))
         nc.scalar.dma_start(out=zw[1:2, :], in_=ln_b.unsqueeze(0))
@@ -133,7 +133,10 @@ def tile_multiheadflashdiff_pb_t_kernel(
         nc.tensor.transpose(ps_w[:], zw[:], identb[:])
 
         def prep_wo_group(g):
-            nc.vector.tensor_copy(out=wo_g[:, g], in_=wo_raw[:, g].rearrange("p t n -> p n t"))
+            nc.vector.tensor_copy(
+                out=wo_g[:, g].rearrange("p (c i) t -> p c t i", i=4),
+                in_=wo_raw[:, g].rearrange("p t (c i) -> p c t i", i=4),
+            )
 
         def prep_wo_quant():
             nc.vector.quantize_mx(
@@ -218,7 +221,7 @@ def tile_multiheadflashdiff_pb_t_kernel(
                 grp_t[i] = gpool.tile([P, 2, P, 4], BF16, tag="grp", name="grp_%d" % i, align_bytes=64)
             dst = grp_t[i][:, g, :, :]
             src = pt_t[(i, g)][:].rearrange("p t r -> p r t")
-            if g == 1 and (i % VD_EVERY == VD_EVERY - 1 or i >= VD_TAIL):
+            if g == 1 and (i % VD_EVERY == VD_EVERY - 1 or i == NT - 2):
                 nc.vector.tensor_scalar(
                     out=dst, in0=src, scalar1=wb[:, 0:1], scalar2=wb[:, 1:2], op0=ALU.mult, op1=ALU.add
                 )
@@ -288,8 +291,11 @@ def tile_multiheadflashdiff_pb_t_kernel(
             if t == 1:
                 nc.vector.tensor_scalar(out=wb[:], in0=ps_w[:, 0:2], scalar1=1.0 - L0, scalar2=None, op0=ALU.mult)
             st_b(t)
+            if t == NT - 1:
+                st_sqrt(t)
             st_d(t - 2, 0)
-            st_sqrt(t)
+            if t < NT - 1:
+                st_sqrt(t)
             st_d(t - 2, 1)
             st_c(t - 1)
             st_t(t - 1)

@@ -84,8 +84,6 @@ def tile_multiheadflashdiff_pb_t_kernel(
             queue = nc.sync if row == 0 else nc.scalar
             queue.dma_start(out=zl[row : row + 1, col : col + 64], in_=v.unsqueeze(0))
         nc.scalar.activation(out=scr[:, 0:1], in_=eps_t[:], func=ACT.Exp)
-        nc.scalar.dma_start(out=zw[0:1, :], in_=ln_w.unsqueeze(0))
-        nc.scalar.dma_start(out=zw[1:2, :], in_=ln_b.unsqueeze(0))
         x1_sb = []
         x2_sb = []
         o_sb = []
@@ -94,14 +92,14 @@ def tile_multiheadflashdiff_pb_t_kernel(
             rows = slice(starts[c], starts[c] + P * J)
             x1c = xpool.tile([P, J, K], BF16, name="x1_%d" % c)
             x2c = xpool.tile([P, J, K], BF16, name="x2_%d" % c)
-            halves = 2 if c == 0 else 1
-            for s in range(halves):
-                cols = slice(s * K // halves, (s + 1) * K // halves)
-                nc.sync.dma_start(out=x2c[:, :, cols], in_=x2_dram[rows, cols].rearrange("(p j) k -> p j k", j=J))
-                nc.sync.dma_start(out=x1c[:, :, cols], in_=x1_dram[rows, cols].rearrange("(p j) k -> p j k", j=J))
+            nc.sync.dma_start(out=x2c[:], in_=x2_dram[rows, :].rearrange("(p j) k -> p j k", j=J))
+            nc.sync.dma_start(out=x1c[:], in_=x1_dram[rows, :].rearrange("(p j) k -> p j k", j=J))
             x1_sb.append(x1c)
             x2_sb.append(x2c)
             o_sb.append(opool.tile([P, J, E], F32, name="o_%d" % c))
+            if c == 1:
+                nc.sync.dma_start(out=zw[0:1, :], in_=ln_w.unsqueeze(0))
+                nc.sync.dma_start(out=zw[1:2, :], in_=ln_b.unsqueeze(0))
             if c == 2:
                 nc.sync.dma_start(
                     out=wo_raw[:].rearrange("p g t n -> p (g t) n"),

@@ -55,7 +55,7 @@ def tile_multiheadflashdiff_pb_t_kernel(
         stat = ctx.enter_context(tc.tile_pool(name="stat", bufs=4))
         gpool = ctx.enter_context(tc.tile_pool(name="gpool", bufs=3))
         qpool = ctx.enter_context(tc.tile_pool(name="qpool", bufs=3))
-        psum = ctx.enter_context(tc.psum_pool(name="psum", bufs=4))
+        psum = ctx.enter_context(tc.psum_pool(name="psum", bufs=5))
 
         eps_t = const.tile([P, 1], F32, name="eps_t")
         nc.vector.memset(eps_t[:], EPS)
@@ -212,14 +212,14 @@ def tile_multiheadflashdiff_pb_t_kernel(
                     h = 4 * g + t
                     nc.tensor.transpose(pt[:, t, :], a_t[i][:, h * D : (h + 1) * D], ident[:])
 
-        def st_d(i, g):
+        def st_d(i, g, on_vector=False):
             if not ok(i):
                 return
             if g == 0:
                 grp_t[i] = gpool.tile([P, 2, P, 4], BF16, tag="grp", name="grp_%d" % i, align_bytes=64)
             dst = grp_t[i][:, g, :, :]
             src = pt_t[(i, g)][:].rearrange("p t r -> p r t")
-            if g == 1 and (i % VD_EVERY == VD_EVERY - 1 or i == NT - 2):
+            if on_vector:
                 nc.vector.tensor_scalar(
                     out=dst, in0=src, scalar1=wb[:, 0:1], scalar2=wb[:, 1:2], op0=ALU.mult, op1=ALU.add
                 )
@@ -254,7 +254,7 @@ def tile_multiheadflashdiff_pb_t_kernel(
                 return
             c, j = where[i]
             if j % 2 == 0:
-                po_t[(c, j // 2)] = psum.tile([P, 2, E], F32, tag="po", bufs=2, name="po_%d" % i)
+                po_t[(c, j // 2)] = psum.tile([P, 2, E], F32, tag="po", bufs=3, name="po_%d" % i)
             po = po_t[(c, j // 2)]
             codes, sc = q_t[i]
             for g in range(2):
@@ -289,39 +289,39 @@ def tile_multiheadflashdiff_pb_t_kernel(
             if t == 1:
                 nc.vector.tensor_scalar(out=wb[:], in0=ps_w[:, 0:2], scalar1=1.0 - L0, scalar2=None, op0=ALU.mult)
             st_b(t)
-            if t == NT - 1:
-                st_sqrt(t)
-            st_d(t - 2, 0)
             if t < NT - 1:
-                st_sqrt(t)
-            st_d(t - 2, 1)
+                st_d(t - 2, 0)
+            st_sqrt(t)
+            if t < NT - 1:
+                st_d(t - 2, 1, (t - 2) % VD_EVERY == 2)
             st_c(t - 1)
+            if t == 4:
+                prep_wo_quant()
+            st_m(t - 4)
             st_t(t - 1)
             if t == 2:
                 prep_wo_group(0)
             if t == 3:
                 prep_wo_group(1)
-            if t == 4:
-                prep_wo_quant()
             st_q(t - 3)
-            st_m(t - 4)
             st_e(t - 5)
-        y, z = NT - 2, NT - 1
+        x, y, z = NT - 3, NT - 2, NT - 1
+        st_d(x, 0, True)
+        st_d(x, 1, True)
+        st_m(z - 3)
         st_c(z)
         st_t(z)
-        st_m(z - 3)
         st_d(y, 0)
-        st_q(z - 2)
         st_d(y, 1)
-        st_m(z - 2)
-        st_e(z - 4)
-        st_d(z, 0)
+        st_q(x)
+        st_m(x)
         st_q(y)
+        st_e(z - 4, nc.scalar.copy)
+        st_d(z, 0)
         st_m(y)
-        st_e(z - 3, nc.scalar.copy)
+        st_d(z, 1, True)
+        st_e(x, nc.scalar.copy)
         st_qh(z, 0)
-        st_d(z, 1)
-        st_e(z - 2, nc.scalar.copy)
         st_qh(z, 1)
         st_m(z)
         st_e(y, nc.scalar.copy)

@@ -295,14 +295,13 @@ def tile_multiheadflashdiff_pb_t_kernel(
             if t < NT - 1:
                 st_d(t - 2, 1, (t - 2) % VD_EVERY == 2)
             st_c(t - 1)
-            if t == 4:
-                prep_wo_quant()
             st_m(t - 4)
             st_t(t - 1)
             if t == 2:
                 prep_wo_group(0)
-            if t == 3:
                 prep_wo_group(1)
+            if t == 3:
+                prep_wo_quant()
             st_q(t - 3)
             st_e(t - 5)
         x, y, z = NT - 3, NT - 2, NT - 1

@@ -142,12 +142,17 @@ def tile_multiheadflashdiff_pb_t_kernel(
             )
 
         a_t = {}
+        a2_t = {}
         ss_t = {}
         r_t = {}
         pt_t = {}
         grp_t = {}
+        whole_t = {}
         q_t = {}
         po_t = {}
+
+        def paired(i):
+            return i < NT - 4
 
         def ok(i):
             return 0 <= i < NT
@@ -156,17 +161,23 @@ def tile_multiheadflashdiff_pb_t_kernel(
             if not ok(i):
                 return
             c, j = where[i]
-            a = apool.tile([P, K], F32, tag="a", name="a_%d" % i)
-            a_t[i] = a
+            k = i % 2
+            if k == 0:
+                a2_t[i // 2] = apool.tile([P, 2, K], F32, tag="a", name="a_%d" % i)
+            a2 = a2_t[i // 2]
+            a_t[i] = a2[:, k, :]
+            if k == 1 and j > 0:
+                return
+            n = 2 if k == 0 and j + 1 < CHUNKS[c] else 1
             pieces = 4 if i == 0 else 1
             w = K // pieces
             for s in range(pieces):
                 cols = slice(s * w, (s + 1) * w)
                 nc.vector.scalar_tensor_tensor(
-                    out=a[:, cols],
-                    in0=x2_sb[c][:, j, cols],
+                    out=a2[:, k : k + n, cols],
+                    in0=x2_sb[c][:, j : j + n, cols],
                     scalar=ps_l[:, 0:1] if i == 0 else neglam[:, 0:1],
-                    in1=x1_sb[c][:, j, cols],
+                    in1=x1_sb[c][:, j : j + n, cols],
                     op0=ALU.mult,
                     op1=ALU.add,
                 )
@@ -215,8 +226,12 @@ def tile_multiheadflashdiff_pb_t_kernel(
         def st_d(i, g, on_vector=False):
             if not ok(i):
                 return
-            if g == 0:
-                grp_t[i] = gpool.tile([P, 2, P, 4], BF16, tag="grp", name="grp_%d" % i, align_bytes=64)
+            if g == 0 and not (paired(i) and i % 2 == 1):
+                n = 2 if paired(i) else 1
+                grp = gpool.tile([P, n, 2, P, 4], BF16, tag="grp", name="grp_%d" % i, align_bytes=64)
+                for k in range(n):
+                    grp_t[i + k] = grp[:, k]
+                    whole_t[i + k] = grp
             dst = grp_t[i][:, g, :, :]
             src = pt_t[(i, g)][:].rearrange("p t r -> p r t")
             if on_vector:
@@ -227,13 +242,16 @@ def tile_multiheadflashdiff_pb_t_kernel(
                 nc.scalar.activation(out=dst, in_=src, func=ACT.Identity, scale=wb[:, 0:1], bias=wb[:, 1:2])
 
         def st_q(i):
-            if not ok(i):
+            if not ok(i) or (paired(i) and i % 2 == 0):
                 return
-            codes = qpool.tile([P, 2 * P], U32, tag="codes", name="codes_%d" % i, align_bytes=64)
-            sc = qpool.tile([P, 2 * P], U8, tag="sc", name="sc_%d" % i, align_bytes=64)
-            q_t[i] = (codes, sc)
+            n = 2 if paired(i) else 1
+            codes = qpool.tile([P, n * 2 * P], U32, tag="codes", name="codes_%d" % i, align_bytes=64)
+            sc = qpool.tile([P, n * 2 * P], U8, tag="sc", name="sc_%d" % i, align_bytes=64)
+            for k in range(n):
+                words = slice(k * 2 * P, (k + 1) * 2 * P)
+                q_t[i - n + 1 + k] = (codes[:, words], sc[:, words])
             nc.vector.quantize_mx(
-                out=codes[:].bitcast(FP8X4), scales=sc[:], in_=grp_t[i][:].rearrange("p g r t -> p (g r t)")
+                out=codes[:].bitcast(FP8X4), scales=sc[:], in_=whole_t[i][:].rearrange("p k g r t -> p (k g r t)")
             )
 
         def st_qh(i, g):
@@ -293,9 +311,13 @@ def tile_multiheadflashdiff_pb_t_kernel(
                 st_d(t - 2, 0)
             st_sqrt(t)
             if t < NT - 1:
-                st_d(t - 2, 1, (t - 2) % VD_EVERY == 2)
+                st_d(t - 2, 1, (t - 2) % VD_EVERY == 3)
             st_c(t - 1)
-            st_m(t - 4)
+            if not paired(t - 4):
+                st_m(t - 4)
+            elif t % 2 == 1:
+                st_m(t - 5)
+                st_m(t - 4)
             st_t(t - 1)
             if t == 2:
                 prep_wo_group(0)

@@ -311,7 +311,7 @@ def tile_multiheadflashdiff_pb_t_kernel(
                 st_d(t - 2, 0)
             st_sqrt(t)
             if t < NT - 1:
-                st_d(t - 2, 1, (t - 2) % VD_EVERY == 3)
+                st_d(t - 2, 1, (t - 2) % VD_EVERY == 3 and t - 2 > 3)
             st_c(t - 1)
             if not paired(t - 4):
                 st_m(t - 4)

import math
from contextlib import ExitStack

import concourse.mybir as mybir
from concourse.masks import make_identity

F32 = mybir.dt.float32
BF16 = mybir.dt.bfloat16
U32 = mybir.dt.uint32
U8 = mybir.dt.uint8
FP8X4 = mybir.dt.float8_e4m3fn_x4
ALU = mybir.AluOpType
ACT = mybir.ActivationFunctionType
AX = mybir.AxisListType

P = 128
H = 8
D = 128
K = H * D
E = 256
TOKENS = 4096
NT = TOKENS // P
L0 = 0.8 - 0.6 * math.exp(-0.3 * 12)
EPS = 1e-8
FLOPS = 2 * TOKENS * K * E
CHUNKS = [1, 1, 1, 1, 2, 2, 4, 4, 4, 4, 4, 2, 1, 1]
VD_EVERY = 4


def tile_multiheadflashdiff_pb_t_kernel(
    tc, attn1, attn2, lambda_q1, lambda_k1, lambda_q2, lambda_k2, ln_w, ln_b, Wo, out
):
    nc = tc.nc
    x1_dram = attn1.rearrange("b s h d -> (b s) (h d)")
    x2_dram = attn2.rearrange("b s h d -> (b s) (h d)")
    out_dram = out.rearrange("b s e -> (b s) e")

    where = []
    starts = []
    t0 = 0
    for c, J in enumerate(CHUNKS):
        starts.append(t0)
        t0 += P * J
        for j in range(J):
            where.append((c, j))
    assert len(where) == NT

    with ExitStack() as ctx:
        ctx.enter_context(tc.manual_schedule())
        const = ctx.enter_context(tc.tile_pool(name="const", bufs=1))
        xpool = ctx.enter_context(tc.tile_pool(name="xpool", bufs=1))
        opool = ctx.enter_context(tc.tile_pool(name="opool", bufs=1))
        apool = ctx.enter_context(tc.tile_pool(name="apool", bufs=4))
        jpool = ctx.enter_context(tc.tile_pool(name="jpool", bufs=2))
        stat = ctx.enter_context(tc.tile_pool(name="stat", bufs=4))
        gpool = ctx.enter_context(tc.tile_pool(name="gpool", bufs=3))
        qpool = ctx.enter_context(tc.tile_pool(name="qpool", bufs=3))
        psum = ctx.enter_context(tc.psum_pool(name="psum", bufs=5))

        eps_t = const.tile([P, 1], F32, name="eps_t")
        nc.vector.memset(eps_t[:], EPS)
        zw = const.tile([P, P], BF16, name="zw")
        nc.vector.memset(zw[:], 0.0)
        zl = const.tile([P, 2 * 64], BF16, name="zl")
        ex = const.tile([P, 1], F32, name="ex")
        nc.vector.memset(ex[:], 0.0)
        nc.vector.memset(ex[32:33, :], 1.0)
        sgn = const.tile([P, P], F32, name="sgn")
        nc.vector.memset(sgn[:], 0.0)
        nc.vector.tensor_scalar(
            out=sgn[32:33, :], in0=sgn[32:33, :], scalar1=-L0, scalar2=None, op0=ALU.add
        )
        nc.vector.memset(sgn[0:2, :], 1.0)
        nc.vector.memset(sgn[0:1, :], -1.0)
        ident = const.tile([P, P], F32, name="ident")
        make_identity(nc, ident[:])
        identb = const.tile([P, P], BF16, name="identb")
        nc.vector.tensor_copy(out=identb[:], in_=ident[:])
        wb = const.tile([P, 2], F32, name="wb")
        scr = const.tile([P, 2], F32, name="scr")

        for n, v in enumerate([lambda_q1, lambda_q2, lambda_k1, lambda_k2]):
            row, col = n % 2, 64 * (n // 2)
            queue = nc.sync if row == 0 else nc.scalar
            queue.dma_start(out=zl[row : row + 1, col : col + 64], in_=v.unsqueeze(0))
        nc.scalar.activation(out=scr[:, 0:1], in_=eps_t[:], func=ACT.Exp)
        x1_sb = []
        x2_sb = []
        o_sb = []
        wo_raw = const.tile([P, 2, 4, E], BF16, name="wo_raw")
        for c, J in enumerate(CHUNKS):
            rows = slice(starts[c], starts[c] + P * J)
            x1c = xpool.tile([P, J, K], BF16, name="x1_%d" % c)
            x2c = xpool.tile([P, J, K], BF16, name="x2_%d" % c)
            nc.sync.dma_start(out=x2c[:], in_=x2_dram[rows, :].rearrange("(p j) k -> p j k", j=J))
            nc.sync.dma_start(out=x1c[:], in_=x1_dram[rows, :].rearrange("(p j) k -> p j k", j=J))
            x1_sb.append(x1c)
            x2_sb.append(x2c)
            o_sb.append(opool.tile([P, J, E], F32, name="o_%d" % c))
            if c == 1:
                nc.sync.dma_start(out=zw[0:1, :], in_=ln_w.unsqueeze(0))
                nc.sync.dma_start(out=zw[1:2, :], in_=ln_b.unsqueeze(0))
            if c == 2:
                nc.sync.dma_start(
                    out=wo_raw[:].rearrange("p g t n -> p (g t) n"),
                    in_=Wo.rearrange("(c p) n -> p c n", p=P),
                )

        prod = const.tile([P, 64], F32, name="prod")
        dots = const.tile([P, 1], F32, name="dots")
        nc.vector.scalar_tensor_tensor(
            out=prod[0:2, :],
            in0=zl[0:2, 0:64],
            scalar=1.0,
            in1=zl[0:2, 64:128],
            op0=ALU.mult,
            op1=ALU.mult,
            accum_out=dots[0:2, :],
        )
        nc.scalar.activation(out=ex[0:2, :], in_=dots[0:2, :], func=ACT.Exp)
        nc.scalar.activation(out=scr[:, 1:2], in_=eps_t[:], func=ACT.Abs_reciprocal_sqrt)
        ps_l = psum.tile([P, 1], F32, tag="tp", name="ps_l")
        nc.tensor.matmul(ps_l[:], lhsT=sgn[:], rhs=ex[:], start=True, stop=True)
        neglam = const.tile([P, 1], F32, name="neglam")

        wo_g = const.tile([P, 2, E, 4], BF16, name="wo_g", align_bytes=64)
        wo_c = const.tile([P, 2 * E], U32, name="wo_c", align_bytes=64)
        wo_s = const.tile([P, 2 * E], U8, name="wo_s", align_bytes=64)

        ps_w = psum.tile([P, P], BF16, tag="tp", name="ps_w")
        nc.tensor.transpose(ps_w[:], zw[:], identb[:])

        def prep_wo_group(g):
            nc.vector.tensor_copy(
                out=wo_g[:, g].rearrange("p (c i) t -> p c t i", i=4),
                in_=wo_raw[:, g].rearrange("p t (c i) -> p c t i", i=4),
            )

        def prep_wo_quant():
            nc.vector.quantize_mx(
                out=wo_c[:].bitcast(FP8X4), scales=wo_s[:], in_=wo_g[:].rearrange("p g n t -> p (g n t)")
            )

        a_t = {}
        a2_t = {}
        ss_t = {}
        r_t = {}
        pt_t = {}
        grp_t = {}
        whole_t = {}
        q_t = {}
        po_t = {}

        def paired(i):
            return i < NT - 4

        def ok(i):
            return 0 <= i < NT

        def st_a(i):
            if not ok(i):
                return
            c, j = where[i]
            k = i % 2
            if k == 0:
                a2_t[i // 2] = apool.tile([P, 2, K], F32, tag="a", name="a_%d" % i)
            a2 = a2_t[i // 2]
            a_t[i] = a2[:, k, :]
            if k == 1 and j > 0:
                return
            n = 2 if k == 0 and j + 1 < CHUNKS[c] else 1
            pieces = 4 if i == 0 else 1
            w = K // pieces
            for s in range(pieces):
                cols = slice(s * w, (s + 1) * w)
                nc.vector.scalar_tensor_tensor(
                    out=a2[:, k : k + n, cols],
                    in0=x2_sb[c][:, j : j + n, cols],
                    scalar=ps_l[:, 0:1] if i == 0 else neglam[:, 0:1],
                    in1=x1_sb[c][:, j : j + n, cols],
                    op0=ALU.mult,
                    op1=ALU.add,
                )

        def st_b(i):
            if not ok(i):
                return
            ss = stat.tile([P, H], F32, tag="ss", name="ss_%d" % i)
            ss_t[i] = ss
            junk = jpool.tile([P, K], BF16, tag="junk", name="junk_%d" % i)
            for h in range(H):
                cols = slice(h * D, (h + 1) * D)
                nc.scalar.activation(
                    out=junk[:, cols], in_=a_t[i][:, cols], func=ACT.Square, accum_out=ss[:, h : h + 1]
                )

        def st_sqrt(i):
            if not ok(i):
                return
            r = stat.tile([P, H], F32, tag="r", name="r_%d" % i)
            r_t[i] = r
            nc.scalar.activation(
                out=r[:], in_=ss_t[i][:], func=ACT.Abs_reciprocal_sqrt, scale=1.0 / D, bias=eps_t[:, 0:1]
            )

        def st_c(i):
            if not ok(i):
                return
            a = a_t[i]
            for h in range(H):
                cols = slice(h * D, (h + 1) * D)
                nc.vector.tensor_scalar(
                    out=a[:, cols], in0=a[:, cols], scalar1=r_t[i][:, h : h + 1], scalar2=None, op0=ALU.mult
                )

        def st_t(i):
            if not ok(i):
                return
            for g in range(2):
                pt = psum.tile([P, 4, P], F32, tag="tp", name="pt_%d_%d" % (i, g))
                pt_t[(i, g)] = pt
                for t in range(4):
                    h = 4 * g + t
                    nc.tensor.transpose(pt[:, t, :], a_t[i][:, h * D : (h + 1) * D], ident[:])

        def st_d(i, g, on_vector=False):
            if not ok(i):
                return
            if g == 0 and not (paired(i) and i % 2 == 1):
                n = 2 if paired(i) else 1
                grp = gpool.tile([P, n, 2, P, 4], BF16, tag="grp", name="grp_%d" % i, align_bytes=64)
                for k in range(n):
                    grp_t[i + k] = grp[:, k]
                    whole_t[i + k] = grp
            dst = grp_t[i][:, g, :, :]
            src = pt_t[(i, g)][:].rearrange("p t r -> p r t")
            if on_vector:
                nc.vector.tensor_scalar(
                    out=dst, in0=src, scalar1=wb[:, 0:1], scalar2=wb[:, 1:2], op0=ALU.mult, op1=ALU.add
                )
            else:
                nc.scalar.activation(out=dst, in_=src, func=ACT.Identity, scale=wb[:, 0:1], bias=wb[:, 1:2])

        def st_q(i):
            if not ok(i) or (paired(i) and i % 2 == 0):
                return
            n = 2 if paired(i) else 1
            codes = qpool.tile([P, n * 2 * P], U32, tag="codes", name="codes_%d" % i, align_bytes=64)
            sc = qpool.tile([P, n * 2 * P], U8, tag="sc", name="sc_%d" % i, align_bytes=64)
            for k in range(n):
                words = slice(k * 2 * P, (k + 1) * 2 * P)
                q_t[i - n + 1 + k] = (codes[:, words], sc[:, words])
            nc.vector.quantize_mx(
                out=codes[:].bitcast(FP8X4), scales=sc[:], in_=whole_t[i][:].rearrange("p k g r t -> p (k g r t)")
            )

        def st_qh(i, g):
            if g == 0:
                q_t[i] = (
                    qpool.tile([P, 2 * P], U32, tag="codes", name="codes_%d" % i, align_bytes=64),
                    qpool.tile([P, 2 * P], U8, tag="sc", name="sc_%d" % i, align_bytes=64),
                )
            codes, sc = q_t[i]
            nc.vector.quantize_mx(
                out=codes[:, g * P : (g + 1) * P].bitcast(FP8X4),
                scales=sc[:, g * P : (g + 1) * P],
                in_=grp_t[i][:, g].rearrange("p r t -> p (r t)"),
            )

        def st_m(i):
            if not ok(i):
                return
            c, j = where[i]
            if j % 2 == 0:
                po_t[(c, j // 2)] = psum.tile([P, 2, E], F32, tag="po", bufs=3, name="po_%d" % i)
            po = po_t[(c, j // 2)]
            codes, sc = q_t[i]
            for g in range(2):
                nc.tensor.matmul_mx(
                    out=po[:, j % 2, :],
                    lhsT=codes[:, g * P : (g + 1) * P].bitcast(FP8X4),
                    lhsT_scale=sc[:, g * P : (g + 1) * P],
                    rhs=wo_c[:, g * E : (g + 1) * E].bitcast(FP8X4),
                    rhs_scale=wo_s[:, g * E : (g + 1) * E],
                    start=(g == 0),
                    stop=(g == 1),
                )

        def st_e(i, copy=nc.vector.tensor_copy):
            if not ok(i):
                return
            c, j = where[i]
            J = CHUNKS[c]
            if j % 2 == 0 and j != J - 1:
                return
            j0 = j - (j % 2)
            n = j - j0 + 1
            copy(out=o_sb[c][:, j0 : j0 + n, :], in_=po_t[(c, j // 2)][:, 0:n, :])
            if j == J - 1:
                rows = slice(starts[c], starts[c] + P * J)
                nc.sync.dma_start(out=out_dram[rows, :].rearrange("(p j) e -> p j e", j=J), in_=o_sb[c][:])

        for t in range(-1, NT):
            st_a(t + 1)
            if t == -1:
                nc.vector.tensor_copy(out=neglam[:], in_=ps_l[:])
            if t == 1:
                nc.vector.tensor_scalar(out=wb[:], in0=ps_w[:, 0:2], scalar1=1.0 - L0, scalar2=None, op0=ALU.mult)
            st_b(t)
            if t < NT - 1:
                st_d(t - 2, 0)
            st_sqrt(t)
            if t < NT - 1:
                st_d(t - 2, 1, (t - 2) % VD_EVERY == 3 and t - 2 > 3)
            st_c(t - 1)
            if not paired(t - 4):
                st_m(t - 4)
            elif t % 2 == 1:
                st_m(t - 5)
                st_m(t - 4)
            st_t(t - 1)
            if t == 2:
                prep_wo_group(0)
                prep_wo_group(1)
            if t == 3:
                prep_wo_quant()
            st_q(t - 3)
            st_e(t - 5)
        x, y, z = NT - 3, NT - 2, NT - 1
        st_d(x, 0, True)
        st_d(x, 1, True)
        st_m(z - 3)
        st_c(z)
        st_t(z)
        st_d(y, 0)
        st_d(y, 1)
        st_q(x)
        st_m(x)
        st_q(y)
        st_e(z - 4, nc.scalar.copy)
        st_d(z, 0)
        st_m(y)
        st_d(z, 1, True)
        st_e(x, nc.scalar.copy)
        st_qh(z, 0)
        st_qh(z, 1)
        st_m(z)
        st_e(y, nc.scalar.copy)
        st_e(z)
